import numpy as np
import ml_dtypes


def mxq(x, axis, fmt="e4m3"):
    dtype, down = {"e4m3": (ml_dtypes.float8_e4m3fn, 7), "e5m2": (ml_dtypes.float8_e5m2, 14)}[fmt]
    v = np.moveaxis(np.asarray(x, np.float32).astype(ml_dtypes.bfloat16).astype(np.float64), axis, -1)
    blocks = v.reshape(v.shape[:-1] + (-1, 32))
    amax = np.abs(blocks).max(-1, keepdims=True)
    byte = np.maximum(np.where(amax > 0, np.frexp(amax)[1] - 1 + 127, 0) - down, 1)
    scale = np.exp2(byte - 127.0)
    codes = (blocks / scale).astype(np.float32).astype(dtype).astype(np.float64)
    return np.moveaxis((codes * scale).reshape(v.shape), -1, axis)


WIDE = False


def mx_kscale(k):
    if not WIDE:
        return np.ones(k)
    levels = np.array([10, -10, 5, -5, 0])
    a = np.random.permutation(np.resize(levels, k // 512 * 4)).reshape(k // 512, 4)
    idx = np.arange(k)
    return np.exp2(a[idx // 512, idx % 128 // 32])


BF16 = ml_dtypes.bfloat16


def bf(x):
    return np.asarray(x, np.float32).astype(BF16)


def f64(x):
    return np.asarray(x).astype(np.float64)


E2M1 = np.array([0.0, 0.5, 1.0, 1.5, 2.0, 3.0, 4.0, 6.0, -0.0, -0.5, -1.0, -1.5, -2.0, -3.0, -4.0, -6.0])


def pack_weight(w, fmt):
    k, n = w.shape
    w = f64(bf(w)).reshape(k // 32, 32, n)
    amax = np.abs(w).max(1)
    if fmt == "e4m3":
        byte = np.frexp(amax)[1] - 1 + 127 - 7
    else:
        mant, ex = np.frexp(amax / 6.0)
        byte = np.where(mant > 0.5, ex, ex - 1) + 127
    byte = np.clip(np.where(amax > 0, byte, 1), 1, 254)
    scaled = (w * np.exp2(127.0 - byte)[:, None, :]).reshape(k, n).astype(np.float32)
    by_word = np.ascontiguousarray(scaled.reshape(k // 512, 128, 4, n).transpose(0, 1, 3, 2))
    if fmt == "e4m3":
        words = by_word.astype(ml_dtypes.float8_e4m3fn).view(np.uint8)
    else:
        c = by_word.astype(ml_dtypes.float4_e2m1fn).view(np.uint8) & 0xF
        words = c[..., 0::2] | (c[..., 1::2] << 4)
    return np.ascontiguousarray(words), np.ascontiguousarray(byte.astype(np.uint8).reshape(k // 512, 16, n))


def unpack_weight(words, scales, fmt):
    g, p, n, _ = words.shape
    if fmt == "e4m3":
        vals = np.ascontiguousarray(words).view(ml_dtypes.float8_e4m3fn).astype(np.float64)
    else:
        nib = np.empty((g, p, n, 4), np.uint8)
        nib[..., 0::2] = words & 0xF
        nib[..., 1::2] = words >> 4
        vals = E2M1[nib]
    vals = vals * np.repeat(np.exp2(scales.astype(np.float64) - 127.0), 8, axis=1)[..., None]
    return vals.transpose(0, 1, 3, 2).reshape(g * 512, n)


M, SP, H, FF, NH = 4096, 3072, 512, 256, 8
EPS = 1.1920929e-07
G = 2


def rms_norm(x, w):
    var = np.mean(np.square(x), axis=-1, keepdims=True)
    return x * (1.0 / np.sqrt(var + EPS)) * w


def silu(v):
    return v / (1.0 + np.exp(-v))


def setup_inputs():
    s, t = mx_kscale(H), mx_kscale(H)
    attn = bf(np.random.standard_normal((M, H)) * 0.25 * s)
    x = bf(np.random.standard_normal((M, H)))
    W_o = np.random.standard_normal((G, H, H)) * 2.0 / np.sqrt(H) / s[None, :, None]
    W_gu = np.random.standard_normal((G, H, 2 * FF)) / np.sqrt(H) / t[None, :, None]
    ln2 = bf((1.0 + 0.1 * np.random.standard_normal((G, H))) * t)
    W_o_words, W_o_scales = pack_weight(W_o.reshape(-1, H), "e4m3")
    W_gu_words, W_gu_scales = pack_weight(W_gu.reshape(-1, 2 * FF), "e4m3")
    return {"attn": attn,
            "x": x,
            "W_o_words": W_o_words,
            "W_o_scales": W_o_scales,
            "W_gu_words": W_gu_words,
            "W_gu_scales": W_gu_scales,
            "ln2": ln2}


def reference(attn, x, W_o_words, W_o_scales, W_gu_words, W_gu_scales, ln2):
    attn, x, ln2 = f64(attn), f64(x), f64(ln2)
    W_o = unpack_weight(W_o_words, W_o_scales, "e4m3").reshape(G, H, H)
    W_gu = unpack_weight(W_gu_words, W_gu_scales, "e4m3").reshape(G, H, 2 * FF)
    o0 = mxq(attn[:SP], 1, "e4m3") @ W_o[0]
    o1 = mxq(attn[SP:], 1, "e4m3") @ W_o[1]
    x_mid = x + np.concatenate([o0, o1], axis=0)
    h0 = rms_norm(x_mid[:SP], ln2[0])
    h1 = rms_norm(x_mid[SP:], ln2[1])
    gu0 = mxq(h0, 1, "e4m3") @ W_gu[0]
    gu1 = mxq(h1, 1, "e4m3") @ W_gu[1]
    gu = np.concatenate([gu0, gu1], axis=0)
    gate, up = np.split(gu, 2, axis=-1)
    return x_mid, silu(gate) * up

@@ -1,0 +1,265 @@
+from contextlib import ExitStack
+
+import concourse.mybir as mybir
+from concourse.masks import make_identity
+
+F32 = mybir.dt.float32
+BF16 = mybir.dt.bfloat16
+U8 = mybir.dt.uint8
+U32 = mybir.dt.uint32
+I32 = mybir.dt.int32
+FP8X4 = mybir.dt.float8_e4m3fn_x4
+ALU = mybir.AluOpType
+ACT = mybir.ActivationFunctionType
+
+P = 128
+PACK = 4
+ROWS = 4096
+ROWS_OF_MODEL = (3072, 1024)
+H = 512
+FF = 256
+EPS = 1.1920929e-07
+TILES = 4
+PAIRS = TILES // 2
+QUADRANTS = 4
+
+FLOPS = 2 * ROWS * H * H + 2 * ROWS * H * 2 * FF
+
+
+def tile_twomodelblockrouted_pb_t_e_kernel(
+    tc, attn, x, W_o_words, W_o_scales, W_gu_words, W_gu_scales, ln2, out_0, out_1
+):
+    nc = tc.nc
+
+    groups = []
+    first_row = 0
+    for model, n_rows in enumerate(ROWS_OF_MODEL):
+        for c in range(n_rows // (P * TILES)):
+            groups.append((model, first_row, n_rows, c))
+        first_row += n_rows
+    n_groups = len(groups)
+
+    def rows_of(dram, g):
+        model, first, n_rows, c = groups[g]
+        by_partition = dram[first : first + n_rows, :].rearrange("(p j) n -> p j n", p=P)
+        return by_partition[:, c * TILES : (c + 1) * TILES, :]
+
+    with ExitStack() as ctx:
+        ctx.enter_context(tc.manual_schedule())
+        consts = ctx.enter_context(tc.tile_pool(name="consts", bufs=1))
+        inputs = ctx.enter_context(tc.tile_pool(name="inputs", bufs=1))
+        two = ctx.enter_context(tc.tile_pool(name="two", bufs=2))
+        three = ctx.enter_context(tc.tile_pool(name="three", bufs=3))
+        four = ctx.enter_context(tc.tile_pool(name="four", bufs=4))
+        flipped_banks = ctx.enter_context(tc.psum_pool(name="flipped_banks", bufs=4))
+        product_banks = ctx.enter_context(tc.psum_pool(name="product_banks", bufs=4))
+
+        wo_planes = consts.tile([P, H], U8, name="wo_planes", align_bytes=64)
+        nc.vector.memset(wo_planes[:].bitcast(I32), 0)
+        wgu_planes = consts.tile([P, H], U8, name="wgu_planes", align_bytes=64)
+        nc.vector.memset(wgu_planes[:].bitcast(I32), 0)
+        neg_half = consts.tile([P, TILES], F32, name="neg_half")
+        nc.vector.memset(neg_half[:], -0.5)
+        warm = consts.tile([P, 1], F32, name="warm")
+        nc.vector.memset(warm[:], 0.0)
+        nc.scalar.activation(out=warm[:], in_=warm[:], func=ACT.Silu)
+        ident = consts.tile([P, P], F32, name="ident")
+        make_identity(nc, ident[:])
+
+        attn_sb = {}
+        x_sb = {}
+        wo_words = {}
+        wgu_words = {}
+        ln2_sb = {}
+
+        def load_rows(dram, g, name):
+            loaded = inputs.tile([P, TILES, H], BF16, name="%s%d" % (name, g))
+            nc.sync.dma_start(out=loaded[:], in_=rows_of(dram, g))
+            return loaded
+
+        def load_planes(dram_scales, planes):
+            for quadrant in range(QUADRANTS):
+                nc.sync.dma_start(
+                    out=planes[32 * quadrant : 32 * quadrant + 8, :].bitcast(I32),
+                    in_=dram_scales[:, 4 * quadrant : 4 * quadrant + 4, :].bitcast(I32),
+                )
+
+        def load_words(dram_words, model, name):
+            loaded = consts.tile([P, H], U32, name="%s%d" % (name, model), align_bytes=64)
+            nc.sync.dma_start(
+                out=loaded[:].bitcast(I32),
+                in_=dram_words[model].rearrange("p n t -> p (n t)").bitcast(I32),
+            )
+            return loaded
+
+        def load_gains(model):
+            loaded = consts.tile([P, H], BF16, name="ln2_sb%d" % model)
+            nc.sync.dma_start(out=loaded[:], in_=ln2[model].partition_broadcast(P))
+            return loaded
+
+        for g in range(n_groups):
+            model = groups[g][0]
+            new_model = model not in wo_words
+            attn_sb[g] = load_rows(attn, g, "attn_sb")
+            if g == 0:
+                load_planes(W_o_scales, wo_planes)
+            if new_model:
+                wo_words[model] = load_words(W_o_words, model, "wo_words")
+            x_sb[g] = load_rows(x, g, "x_sb")
+            if g == 0:
+                load_planes(W_gu_scales, wgu_planes)
+            if new_model:
+                wgu_words[model] = load_words(W_gu_words, model, "wgu_words")
+                ln2_sb[model] = load_gains(model)
+
+        def transpose_pair(row_tiles, pair):
+            flipped = flipped_banks.tile([P, 2, 2, P], F32, name="flipped", tag="flipped")
+            for i in range(2):
+                words = row_tiles[:, 2 * pair + i, :].bitcast(F32)
+                for u in range(2):
+                    nc.tensor.transpose(flipped[:, i, u, :], words[:, u : H // 2 : 2], ident[:])
+            return flipped
+
+        def regroup_pair(flipped, grouped, pair):
+            nc.scalar.copy(
+                out=grouped[:, 2 * pair : 2 * pair + 2, :, :].bitcast(F32),
+                in_=flipped[:].rearrange("p i u r -> p i r u"),
+            )
+
+        def quantise(grouped, name):
+            codes = two.tile([P, TILES * P], U32, name=name + "_codes", align_bytes=64)
+            scales = two.tile([P, TILES * P], U8, name=name + "_scales", align_bytes=64)
+            nc.vector.quantize_mx(
+                out=codes[:].bitcast(FP8X4),
+                scales=scales[:],
+                in_=grouped[:].rearrange("p j r t -> p (j r t)"),
+            )
+            return codes, scales
+
+        def mx_product(quantised, j, weight_words, planes, model):
+            codes, scales = quantised
+            product = product_banks.tile([P, H], F32, name="product", tag="product")
+            tile_j = slice(j * P, (j + 1) * P)
+            nc.tensor.matmul_mx(
+                out=product[:],
+                lhsT=codes[:, tile_j].bitcast(FP8X4),
+                lhsT_scale=scales[:, tile_j],
+                rhs=weight_words[model][:].bitcast(FP8X4),
+                rhs_scale=planes[4 * model : P, :],
+                start=True,
+                stop=True,
+            )
+            return product
+
+        attn_flipped = {}
+        attn_grouped = {}
+        attn_q = {}
+        o_ps = {}
+        x_mid = {}
+        sumsq = {}
+        rstd = {}
+        h_grouped = {}
+        h_q = {}
+        gu_ps = {}
+        silu_gate = {}
+
+        def transpose_attn(g):
+            attn_flipped[g] = [transpose_pair(attn_sb[g], pair) for pair in range(PAIRS)]
+
+        def regroup_attn(g):
+            attn_grouped[g] = two.tile([P, TILES, P, PACK], BF16, name="attn_grouped", align_bytes=64)
+            for pair in range(PAIRS):
+                regroup_pair(attn_flipped[g][pair], attn_grouped[g], pair)
+
+        def first_products(g):
+            model = groups[g][0]
+            o_ps[g] = [mx_product(attn_q[g], j, wo_words, wo_planes, model) for j in range(TILES)]
+            x_mid[g] = four.tile([P, TILES, H], F32, name="x_mid")
+            sumsq[g] = three.tile([P, TILES], F32, name="sumsq")
+
+        def add_residual(g, j):
+            nc.vector.tensor_tensor(
+                out=x_mid[g][:, j, :], in0=o_ps[g][j][:], in1=x_sb[g][:, j, :], op=ALU.add
+            )
+
+        def sum_squares(g, j):
+            squares = four.tile([P, H], BF16, name="squares")
+            nc.scalar.activation(
+                out=squares[:], in_=x_mid[g][:, j, :], func=ACT.Square,
+                accum_out=sumsq[g][:, j : j + 1],
+            )
+
+        def reciprocal_rms(g):
+            mean_eps = three.tile([P, TILES], F32, name="mean_eps")
+            nc.gpsimd.tensor_scalar(
+                out=mean_eps[:], in0=sumsq[g][:], scalar1=1.0 / H, scalar2=EPS,
+                op0=ALU.mult, op1=ALU.add,
+            )
+            rstd[g] = three.tile([P, TILES], F32, name="rstd")
+            nc.gpsimd.tensor_tensor(out=rstd[g][:], in0=mean_eps[:], in1=neg_half[:], op=ALU.pow)
+
+        def normalise_transpose_regroup(g):
+            model = groups[g][0]
+            h = two.tile([P, TILES, H], BF16, name="h")
+            h_grouped[g] = two.tile([P, TILES, P, PACK], BF16, name="h_grouped", align_bytes=64)
+            for pair in range(PAIRS):
+                for j in range(2 * pair, 2 * pair + 2):
+                    nc.vector.scalar_tensor_tensor(
+                        out=h[:, j, :], in0=x_mid[g][:, j, :], scalar=rstd[g][:, j : j + 1],
+                        in1=ln2_sb[model][:], op0=ALU.mult, op1=ALU.mult,
+                    )
+                regroup_pair(transpose_pair(h, pair), h_grouped[g], pair)
+
+        def second_product(g, j):
+            model = groups[g][0]
+            gu_ps[g].append(mx_product(h_q[g], j, wgu_words, wgu_planes, model))
+
+        def silu_of_gate(g, j):
+            nc.scalar.activation(out=silu_gate[g][:, j, :], in_=gu_ps[g][j][:, 0:FF], func=ACT.Silu)
+
+        def gate_times_up(g):
+            h_mlp = three.tile([P, TILES, FF], F32, name="h_mlp")
+            for j in range(TILES):
+                nc.vector.tensor_tensor(
+                    out=h_mlp[:, j, :], in0=silu_gate[g][:, j, :], in1=gu_ps[g][j][:, FF : 2 * FF],
+                    op=ALU.mult,
+                )
+            nc.sync.dma_start(out=rows_of(out_1, g), in_=h_mlp[:])
+
+        def valid(g):
+            return 0 <= g < n_groups
+
+        transpose_attn(0)
+        regroup_attn(0)
+        attn_q[0] = quantise(attn_grouped[0], "attn")
+        transpose_attn(1)
+
+        for t in range(n_groups + 2):
+            if valid(t):
+                first_products(t)
+            if valid(t - 2):
+                h_q[t - 2] = quantise(h_grouped[t - 2], "h")
+                gu_ps[t - 2] = []
+                silu_gate[t - 2] = two.tile([P, TILES, FF], F32, name="silu_gate")
+            if valid(t + 1):
+                regroup_attn(t + 1)
+            for j in range(TILES):
+                if valid(t):
+                    add_residual(t, j)
+                if valid(t - 2):
+                    second_product(t - 2, j)
+                if valid(t):
+                    sum_squares(t, j)
+                if valid(t - 2):
+                    silu_of_gate(t - 2, j)
+            if valid(t):
+                nc.sync.dma_start(out=rows_of(out_0, t), in_=x_mid[t][:])
+                reciprocal_rms(t)
+            if valid(t + 2):
+                transpose_attn(t + 2)
+            if valid(t - 1):
+                normalise_transpose_regroup(t - 1)
+            if valid(t + 1):
+                attn_q[t + 1] = quantise(attn_grouped[t + 1], "attn")
+            if valid(t - 2):
+                gate_times_up(t - 2)

@@ -19,8 +19,7 @@ ROWS_OF_MODEL = (3072, 1024)
 H = 512
 FF = 256
 EPS = 1.1920929e-07
-TILES = 4
-PAIRS = TILES // 2
+TILES = 2
 QUADRANTS = 4
 
 FLOPS = 2 * ROWS * H * H + 2 * ROWS * H * 2 * FF
@@ -31,38 +30,47 @@ def tile_twomodelblockrouted_pb_t_e_kernel(
 ):
     nc = tc.nc
 
-    groups = []
-    first_row = 0
+    first_row_of_model = (0, ROWS_OF_MODEL[0])
+    blocks = []
     for model, n_rows in enumerate(ROWS_OF_MODEL):
-        for c in range(n_rows // (P * TILES)):
-            groups.append((model, first_row, n_rows, c))
-        first_row += n_rows
-    n_groups = len(groups)
+        for tile in range(0, n_rows // P, 2):
+            at_an_end = tile == 0 if model == 0 else tile == n_rows // P - 2
+            if at_an_end:
+                blocks += [(model, tile, 1), (model, tile + 1, 1)]
+            else:
+                blocks.append((model, tile, 2))
+    n_blocks = len(blocks)
 
-    def rows_of(dram, g):
-        model, first, n_rows, c = groups[g]
+    def rows_of(dram, model, tile, n_tiles):
+        first, n_rows = first_row_of_model[model], ROWS_OF_MODEL[model]
         by_partition = dram[first : first + n_rows, :].rearrange("(p j) n -> p j n", p=P)
-        return by_partition[:, c * TILES : (c + 1) * TILES, :]
+        return by_partition[:, tile : tile + n_tiles, :]
 
     with ExitStack() as ctx:
         ctx.enter_context(tc.manual_schedule())
         consts = ctx.enter_context(tc.tile_pool(name="consts", bufs=1))
-        inputs = ctx.enter_context(tc.tile_pool(name="inputs", bufs=1))
-        two = ctx.enter_context(tc.tile_pool(name="two", bufs=2))
-        three = ctx.enter_context(tc.tile_pool(name="three", bufs=3))
+        whole = ctx.enter_context(tc.tile_pool(name="whole", bufs=1))
         four = ctx.enter_context(tc.tile_pool(name="four", bufs=4))
         flipped_banks = ctx.enter_context(tc.psum_pool(name="flipped_banks", bufs=4))
         product_banks = ctx.enter_context(tc.psum_pool(name="product_banks", bufs=4))
 
+        ln2_rows = consts.tile([P, H], BF16, name="ln2_rows")
+        pick = consts.tile([P, 2, P], BF16, name="pick")
+        warm = consts.tile([P, 1], F32, name="warm")
+        nc.vector.memset(warm[:], 0.0)
+        nc.scalar.activation(out=warm[:], in_=warm[:], func=ACT.Silu)
         wo_planes = consts.tile([P, H], U8, name="wo_planes", align_bytes=64)
         nc.vector.memset(wo_planes[:].bitcast(I32), 0)
         wgu_planes = consts.tile([P, H], U8, name="wgu_planes", align_bytes=64)
         nc.vector.memset(wgu_planes[:].bitcast(I32), 0)
+        nc.vector.memset(ln2_rows[:], 0.0)
+        nc.vector.memset(pick[:], 0.0)
+        for model in range(2):
+            row = 32 * model
+            nc.vector.memset(pick[row : row + 1, model, :], 1.0)
+            nc.scalar.dma_start(out=ln2_rows[row : row + 1, :], in_=ln2[model : model + 1, :])
         neg_half = consts.tile([P, TILES], F32, name="neg_half")
         nc.vector.memset(neg_half[:], -0.5)
-        warm = consts.tile([P, 1], F32, name="warm")
-        nc.vector.memset(warm[:], 0.0)
-        nc.scalar.activation(out=warm[:], in_=warm[:], func=ACT.Silu)
         ident = consts.tile([P, P], F32, name="ident")
         make_identity(nc, ident[:])
 
@@ -70,12 +78,15 @@ def tile_twomodelblockrouted_pb_t_e_kernel(
         x_sb = {}
         wo_words = {}
         wgu_words = {}
-        ln2_sb = {}
 
-        def load_rows(dram, g, name):
-            loaded = inputs.tile([P, TILES, H], BF16, name="%s%d" % (name, g))
-            nc.sync.dma_start(out=loaded[:], in_=rows_of(dram, g))
-            return loaded
+        def load_rows(dram, into, first, n, name):
+            model, tile, unused_size = blocks[first]
+            n_tiles = sum(size for unused_model, unused_tile, size in blocks[first : first + n])
+            loaded = whole.tile([P, n_tiles, H], BF16, name="%s%d" % (name, first))
+            nc.sync.dma_start(out=loaded[:], in_=rows_of(dram, model, tile, n_tiles))
+            for u in range(first, first + n):
+                offset = blocks[u][1] - tile
+                into[u] = loaded[:, offset : offset + blocks[u][2], :]
 
         def load_planes(dram_scales, planes):
             for quadrant in range(QUADRANTS):
@@ -92,174 +103,208 @@ def tile_twomodelblockrouted_pb_t_e_kernel(
             )
             return loaded
 
-        def load_gains(model):
-            loaded = consts.tile([P, H], BF16, name="ln2_sb%d" % model)
-            nc.sync.dma_start(out=loaded[:], in_=ln2[model].partition_broadcast(P))
-            return loaded
+        load_rows(attn, attn_sb, 0, 1, "attn_sb")
+        load_planes(W_o_scales, wo_planes)
+        wo_words[0] = load_words(W_o_words, 0, "wo_words")
+        load_rows(attn, attn_sb, 1, 1, "attn_sb")
+        load_rows(x, x_sb, 0, 2, "x_sb")
+        load_rows(attn, attn_sb, 2, 1, "attn_sb")
+        load_rows(x, x_sb, 2, 1, "x_sb")
+        load_planes(W_gu_scales, wgu_planes)
+        wgu_words[0] = load_words(W_gu_words, 0, "wgu_words")
+        load_rows(attn, attn_sb, 3, 2, "attn_sb")
+        load_rows(x, x_sb, 3, 2, "x_sb")
+        for first, n in ((5, 2), (7, 2), (9, 2), (11, 2), (13, 2), (15, 3)):
+            load_rows(attn, attn_sb, first, n, "attn_sb")
+            load_rows(x, x_sb, first, n, "x_sb")
+            if first == 9:
+                wo_words[1] = load_words(W_o_words, 1, "wo_words")
+                wgu_words[1] = load_words(W_gu_words, 1, "wgu_words")
 
-        for g in range(n_groups):
-            model = groups[g][0]
-            new_model = model not in wo_words
-            attn_sb[g] = load_rows(attn, g, "attn_sb")
-            if g == 0:
-                load_planes(W_o_scales, wo_planes)
-            if new_model:
-                wo_words[model] = load_words(W_o_words, model, "wo_words")
-            x_sb[g] = load_rows(x, g, "x_sb")
-            if g == 0:
-                load_planes(W_gu_scales, wgu_planes)
-            if new_model:
-                wgu_words[model] = load_words(W_gu_words, model, "wgu_words")
-                ln2_sb[model] = load_gains(model)
-
-        def transpose_pair(row_tiles, pair):
-            flipped = flipped_banks.tile([P, 2, 2, P], F32, name="flipped", tag="flipped")
-            for i in range(2):
-                words = row_tiles[:, 2 * pair + i, :].bitcast(F32)
+        def transpose_tiles(row_tiles):
+            n = row_tiles.shape[1]
+            flipped = flipped_banks.tile([P, n, 2, P], F32, name="flipped", tag="flipped")
+            for i in range(n):
+                words = row_tiles[:, i, :].bitcast(F32)
                 for u in range(2):
                     nc.tensor.transpose(flipped[:, i, u, :], words[:, u : H // 2 : 2], ident[:])
             return flipped
 
-        def regroup_pair(flipped, grouped, pair):
+        def regroup(flipped):
+            n = flipped.shape[1]
+            grouped = four.tile([P, n, P, PACK], BF16, name="grouped", align_bytes=64)
             nc.scalar.copy(
-                out=grouped[:, 2 * pair : 2 * pair + 2, :, :].bitcast(F32),
-                in_=flipped[:].rearrange("p i u r -> p i r u"),
+                out=grouped[:].bitcast(F32), in_=flipped[:].rearrange("p i u r -> p i r u")
             )
+            return grouped
 
-        def quantise(grouped, name):
-            codes = two.tile([P, TILES * P], U32, name=name + "_codes", align_bytes=64)
-            scales = two.tile([P, TILES * P], U8, name=name + "_scales", align_bytes=64)
+        def quantise(grouped):
+            n = grouped.shape[1]
+            codes = four.tile([P, n * P], U32, name="codes", align_bytes=64)
+            scales = four.tile([P, n * P], U8, name="scales", align_bytes=64)
             nc.vector.quantize_mx(
                 out=codes[:].bitcast(FP8X4),
                 scales=scales[:],
-                in_=grouped[:].rearrange("p j r t -> p (j r t)"),
+                in_=grouped[:].rearrange("p i r t -> p (i r t)"),
             )
             return codes, scales
 
-        def mx_product(quantised, j, weight_words, planes, model):
+        def mx_product(out, quantised, i, weight_words, planes, model, columns):
             codes, scales = quantised
-            product = product_banks.tile([P, H], F32, name="product", tag="product")
-            tile_j = slice(j * P, (j + 1) * P)
+            tile_i = slice(i * P, (i + 1) * P)
             nc.tensor.matmul_mx(
-                out=product[:],
-                lhsT=codes[:, tile_j].bitcast(FP8X4),
-                lhsT_scale=scales[:, tile_j],
-                rhs=weight_words[model][:].bitcast(FP8X4),
-                rhs_scale=planes[4 * model : P, :],
+                out=out,
+                lhsT=codes[:, tile_i].bitcast(FP8X4),
+                lhsT_scale=scales[:, tile_i],
+                rhs=weight_words[model][:, columns].bitcast(FP8X4),
+                rhs_scale=planes[4 * model : P, columns],
                 start=True,
                 stop=True,
             )
-            return product
 
-        attn_flipped = {}
+        ln2_sb = {}
+        flipped = {}
         attn_grouped = {}
         attn_q = {}
         o_ps = {}
         x_mid = {}
         sumsq = {}
         rstd = {}
+        h = {}
+        h_flipped = {}
         h_grouped = {}
         h_q = {}
-        gu_ps = {}
+        gate_ps = {}
+        up_ps = {}
         silu_gate = {}
 
-        def transpose_attn(g):
-            attn_flipped[g] = [transpose_pair(attn_sb[g], pair) for pair in range(PAIRS)]
-
-        def regroup_attn(g):
-            attn_grouped[g] = two.tile([P, TILES, P, PACK], BF16, name="attn_grouped", align_bytes=64)
-            for pair in range(PAIRS):
-                regroup_pair(attn_flipped[g][pair], attn_grouped[g], pair)
-
-        def first_products(g):
-            model = groups[g][0]
-            o_ps[g] = [mx_product(attn_q[g], j, wo_words, wo_planes, model) for j in range(TILES)]
-            x_mid[g] = four.tile([P, TILES, H], F32, name="x_mid")
-            sumsq[g] = three.tile([P, TILES], F32, name="sumsq")
-
-        def add_residual(g, j):
-            nc.vector.tensor_tensor(
-                out=x_mid[g][:, j, :], in0=o_ps[g][j][:], in1=x_sb[g][:, j, :], op=ALU.add
+        def spread_ln2(model):
+            spread = flipped_banks.tile([P, H], F32, name="spread", tag="flipped")
+            nc.tensor.matmul(
+                out=spread[:], lhsT=pick[:, model, :], rhs=ln2_rows[:], start=True, stop=True
             )
+            ln2_sb[model] = consts.tile([P, H], BF16, name="ln2_sb%d" % model)
+            nc.scalar.copy(out=ln2_sb[model][:], in_=spread[:])
 
-        def sum_squares(g, j):
-            squares = four.tile([P, H], BF16, name="squares")
-            nc.scalar.activation(
-                out=squares[:], in_=x_mid[g][:, j, :], func=ACT.Square,
-                accum_out=sumsq[g][:, j : j + 1],
-            )
+        def transpose_attn(u):
+            flipped[u] = transpose_tiles(attn_sb[u])
 
-        def reciprocal_rms(g):
-            mean_eps = three.tile([P, TILES], F32, name="mean_eps")
+        def regroup_attn(u):
+            attn_grouped[u] = regroup(flipped[u])
+
+        def quantise_attn(u):
+            attn_q[u] = quantise(attn_grouped[u])
+
+        def first_products(u):
+            o_ps[u] = []
+            for i in range(blocks[u][2]):
+                o = product_banks.tile([P, H], F32, name="o", tag="product")
+                mx_product(o[:], attn_q[u], i, wo_words, wo_planes, blocks[u][0], slice(0, H))
+                o_ps[u].append(o)
+
+        def add_residual(u):
+            model, tile, n = blocks[u]
+            x_mid[u] = whole.tile([P, n, H], F32, name="x_mid%d" % u)
+            for i in range(n):
+                nc.vector.tensor_tensor(
+                    out=x_mid[u][:, i, :], in0=o_ps[u][i][:], in1=x_sb[u][:, i, :], op=ALU.add
+                )
+            nc.sync.dma_start(out=rows_of(out_0, model, tile, n), in_=x_mid[u][:])
+
+        def sum_squares(u):
+            n = blocks[u][2]
+            sumsq[u] = four.tile([P, n], F32, name="sumsq")
+            for i in range(n):
+                squares = four.tile([P, H], BF16, name="squares")
+                nc.scalar.activation(
+                    out=squares[:], in_=x_mid[u][:, i, :], func=ACT.Square,
+                    accum_out=sumsq[u][:, i : i + 1],
+                )
+
+        def reciprocal_rms(u):
+            n = blocks[u][2]
+            mean_eps = four.tile([P, n], F32, name="mean_eps")
             nc.gpsimd.tensor_scalar(
-                out=mean_eps[:], in0=sumsq[g][:], scalar1=1.0 / H, scalar2=EPS,
+                out=mean_eps[:], in0=sumsq[u][:], scalar1=1.0 / H, scalar2=EPS,
                 op0=ALU.mult, op1=ALU.add,
             )
-            rstd[g] = three.tile([P, TILES], F32, name="rstd")
-            nc.gpsimd.tensor_tensor(out=rstd[g][:], in0=mean_eps[:], in1=neg_half[:], op=ALU.pow)
+            rstd[u] = four.tile([P, n], F32, name="rstd")
+            nc.gpsimd.tensor_tensor(
+                out=rstd[u][:], in0=mean_eps[:], in1=neg_half[:, 0:n], op=ALU.pow
+            )
 
-        def normalise_transpose_regroup(g):
-            model = groups[g][0]
-            h = two.tile([P, TILES, H], BF16, name="h")
-            h_grouped[g] = two.tile([P, TILES, P, PACK], BF16, name="h_grouped", align_bytes=64)
-            for pair in range(PAIRS):
-                for j in range(2 * pair, 2 * pair + 2):
-                    nc.vector.scalar_tensor_tensor(
-                        out=h[:, j, :], in0=x_mid[g][:, j, :], scalar=rstd[g][:, j : j + 1],
-                        in1=ln2_sb[model][:], op0=ALU.mult, op1=ALU.mult,
-                    )
-                regroup_pair(transpose_pair(h, pair), h_grouped[g], pair)
-
-        def second_product(g, j):
-            model = groups[g][0]
-            gu_ps[g].append(mx_product(h_q[g], j, wgu_words, wgu_planes, model))
-
-        def silu_of_gate(g, j):
-            nc.scalar.activation(out=silu_gate[g][:, j, :], in_=gu_ps[g][j][:, 0:FF], func=ACT.Silu)
-
-        def gate_times_up(g):
-            h_mlp = three.tile([P, TILES, FF], F32, name="h_mlp")
-            for j in range(TILES):
-                nc.vector.tensor_tensor(
-                    out=h_mlp[:, j, :], in0=silu_gate[g][:, j, :], in1=gu_ps[g][j][:, FF : 2 * FF],
-                    op=ALU.mult,
+        def normalise(u):
+            model, unused_tile, n = blocks[u]
+            h[u] = four.tile([P, n, H], BF16, name="h")
+            for i in range(n):
+                nc.vector.scalar_tensor_tensor(
+                    out=h[u][:, i, :],
+                    in0=x_mid[u][:, i, :],
+                    scalar=rstd[u][:, i : i + 1],
+                    in1=ln2_sb[model][:],
+                    op0=ALU.mult, op1=ALU.mult,
                 )
-            nc.sync.dma_start(out=rows_of(out_1, g), in_=h_mlp[:])
 
-        def valid(g):
-            return 0 <= g < n_groups
+        def transpose_h(u):
+            h_flipped[u] = transpose_tiles(h[u])
+
+        def regroup_h(u):
+            h_grouped[u] = regroup(h_flipped[u])
+
+        def quantise_h(u):
+            h_q[u] = quantise(h_grouped[u])
+
+        def second_products(u):
+            model, unused_tile, n = blocks[u]
+            gate_ps[u] = product_banks.tile([P, n, FF], F32, name="gate", tag="product")
+            up_ps[u] = product_banks.tile([P, n, FF], F32, name="up", tag="product")
+            for out, columns in ((gate_ps[u], slice(0, FF)), (up_ps[u], slice(FF, 2 * FF))):
+                for i in range(n):
+                    mx_product(out[:, i, :], h_q[u], i, wgu_words, wgu_planes, model, columns)
+
+        def silu_of_gate(u):
+            silu_gate[u] = four.tile([P, blocks[u][2], FF], F32, name="silu_gate")
+            nc.scalar.activation(out=silu_gate[u][:], in_=gate_ps[u][:], func=ACT.Silu)
+
+        def gate_times_up(u):
+            model, tile, n = blocks[u]
+            h_mlp = whole.tile([P, n, FF], F32, name="h_mlp%d" % u)
+            nc.vector.tensor_tensor(out=h_mlp[:], in0=silu_gate[u][:], in1=up_ps[u][:], op=ALU.mult)
+            nc.sync.dma_start(out=rows_of(out_1, model, tile, n), in_=h_mlp[:])
+
+        def valid(u):
+            return 0 <= u < n_blocks
 
         transpose_attn(0)
         regroup_attn(0)
-        attn_q[0] = quantise(attn_grouped[0], "attn")
+        quantise_attn(0)
         transpose_attn(1)
+        regroup_attn(1)
+        first_products(0)
+        for model in range(2):
+            spread_ln2(model)
 
-        for t in range(n_groups + 2):
-            if valid(t):
-                first_products(t)
+        for t in range(n_blocks + 3):
             if valid(t - 2):
-                h_q[t - 2] = quantise(h_grouped[t - 2], "h")
-                gu_ps[t - 2] = []
-                silu_gate[t - 2] = two.tile([P, TILES, FF], F32, name="silu_gate")
-            if valid(t + 1):
-                regroup_attn(t + 1)
-            for j in range(TILES):
-                if valid(t):
-                    add_residual(t, j)
-                if valid(t - 2):
-                    second_product(t - 2, j)
-                if valid(t):
-                    sum_squares(t, j)
-                if valid(t - 2):
-                    silu_of_gate(t - 2, j)
-            if valid(t):
-                nc.sync.dma_start(out=rows_of(out_0, t), in_=x_mid[t][:])
-                reciprocal_rms(t)
+                regroup_h(t - 2)
+            if valid(t - 3):
+                quantise_h(t - 3)
+                second_products(t - 3)
             if valid(t + 2):
                 transpose_attn(t + 2)
-            if valid(t - 1):
-                normalise_transpose_regroup(t - 1)
+            if valid(t):
+                add_residual(t)
+                sum_squares(t)
+                reciprocal_rms(t)
+            if valid(t - 3):
+                silu_of_gate(t - 3)
             if valid(t + 1):
-                attn_q[t + 1] = quantise(attn_grouped[t + 1], "attn")
-            if valid(t - 2):
-                gate_times_up(t - 2)
+                quantise_attn(t + 1)
+                first_products(t + 1)
+            if valid(t + 2):
+                regroup_attn(t + 2)
+            if valid(t - 1):
+                normalise(t - 1)
+                transpose_h(t - 1)
+            if valid(t - 3):
+                gate_times_up(t - 3)

@@ -20,6 +20,7 @@ H = 512
 FF = 256
 EPS = 1.1920929e-07
 TILES = 2
+WARM_UP = 4
 QUADRANTS = 4
 
 FLOPS = 2 * ROWS * H * H + 2 * ROWS * H * 2 * FF
@@ -31,14 +32,10 @@ def tile_twomodelblockrouted_pb_t_e_kernel(
     nc = tc.nc
 
     first_row_of_model = (0, ROWS_OF_MODEL[0])
-    blocks = []
+    blocks = [(0, 0, 1), (0, 1, 1)]
     for model, n_rows in enumerate(ROWS_OF_MODEL):
-        for tile in range(0, n_rows // P, 2):
-            at_an_end = tile == 0 if model == 0 else tile == n_rows // P - 2
-            if at_an_end:
-                blocks += [(model, tile, 1), (model, tile + 1, 1)]
-            else:
-                blocks.append((model, tile, 2))
+        for tile in range(2 if model == 0 else 0, n_rows // P, 2):
+            blocks.append((model, tile, 2))
     n_blocks = len(blocks)
 
     def rows_of(dram, model, tile, n_tiles):
@@ -51,24 +48,27 @@ def tile_twomodelblockrouted_pb_t_e_kernel(
         consts = ctx.enter_context(tc.tile_pool(name="consts", bufs=1))
         whole = ctx.enter_context(tc.tile_pool(name="whole", bufs=1))
         four = ctx.enter_context(tc.tile_pool(name="four", bufs=4))
-        flipped_banks = ctx.enter_context(tc.psum_pool(name="flipped_banks", bufs=4))
-        product_banks = ctx.enter_context(tc.psum_pool(name="product_banks", bufs=4))
+        eight = ctx.enter_context(tc.tile_pool(name="eight", bufs=8))
+        flipped_banks = ctx.enter_context(tc.psum_pool(name="flipped_banks", bufs=2))
+        o_banks = ctx.enter_context(tc.psum_pool(name="o_banks", bufs=3))
+        gu_banks = ctx.enter_context(tc.psum_pool(name="gu_banks", bufs=3))
 
         ln2_rows = consts.tile([P, H], BF16, name="ln2_rows")
         pick = consts.tile([P, 2, P], BF16, name="pick")
         warm = consts.tile([P, 1], F32, name="warm")
         nc.vector.memset(warm[:], 0.0)
         nc.scalar.activation(out=warm[:], in_=warm[:], func=ACT.Silu)
+        zeros = consts.tile([P, H], BF16, name="zeros")
+        nc.vector.memset(zeros[:].bitcast(F32), 0.0)
         wo_planes = consts.tile([P, H], U8, name="wo_planes", align_bytes=64)
         nc.vector.memset(wo_planes[:].bitcast(I32), 0)
         wgu_planes = consts.tile([P, H], U8, name="wgu_planes", align_bytes=64)
         nc.vector.memset(wgu_planes[:].bitcast(I32), 0)
-        nc.vector.memset(ln2_rows[:], 0.0)
+        nc.vector.memset(ln2_rows[:].bitcast(F32), 0.0)
         nc.vector.memset(pick[:], 0.0)
         for model in range(2):
             row = 32 * model
             nc.vector.memset(pick[row : row + 1, model, :], 1.0)
-            nc.scalar.dma_start(out=ln2_rows[row : row + 1, :], in_=ln2[model : model + 1, :])
         neg_half = consts.tile([P, TILES], F32, name="neg_half")
         nc.vector.memset(neg_half[:], -0.5)
         ident = consts.tile([P, P], F32, name="ident")
@@ -104,19 +104,19 @@ def tile_twomodelblockrouted_pb_t_e_kernel(
             return loaded
 
         load_rows(attn, attn_sb, 0, 1, "attn_sb")
+        load_rows(attn, attn_sb, 1, 1, "attn_sb")
         load_planes(W_o_scales, wo_planes)
         wo_words[0] = load_words(W_o_words, 0, "wo_words")
-        load_rows(attn, attn_sb, 1, 1, "attn_sb")
         load_rows(x, x_sb, 0, 2, "x_sb")
+        nc.sync.dma_start(out=ln2_rows[0:64:32, :], in_=ln2[:, :])
         load_rows(attn, attn_sb, 2, 1, "attn_sb")
         load_rows(x, x_sb, 2, 1, "x_sb")
-        load_planes(W_gu_scales, wgu_planes)
-        wgu_words[0] = load_words(W_gu_words, 0, "wgu_words")
-        load_rows(attn, attn_sb, 3, 2, "attn_sb")
-        load_rows(x, x_sb, 3, 2, "x_sb")
-        for first, n in ((5, 2), (7, 2), (9, 2), (11, 2), (13, 2), (15, 3)):
-            load_rows(attn, attn_sb, first, n, "attn_sb")
-            load_rows(x, x_sb, first, n, "x_sb")
+        for first in range(3, n_blocks, 2):
+            load_rows(attn, attn_sb, first, 2, "attn_sb")
+            if first == 3:
+                load_planes(W_gu_scales, wgu_planes)
+                wgu_words[0] = load_words(W_gu_words, 0, "wgu_words")
+            load_rows(x, x_sb, first, 2, "x_sb")
             if first == 9:
                 wo_words[1] = load_words(W_o_words, 1, "wo_words")
                 wgu_words[1] = load_words(W_gu_words, 1, "wgu_words")
@@ -184,7 +184,7 @@ def tile_twomodelblockrouted_pb_t_e_kernel(
                 out=spread[:], lhsT=pick[:, model, :], rhs=ln2_rows[:], start=True, stop=True
             )
             ln2_sb[model] = consts.tile([P, H], BF16, name="ln2_sb%d" % model)
-            nc.scalar.copy(out=ln2_sb[model][:], in_=spread[:])
+            nc.vector.tensor_copy(out=ln2_sb[model][:], in_=spread[:])
 
         def transpose_attn(u):
             flipped[u] = transpose_tiles(attn_sb[u])
@@ -198,7 +198,7 @@ def tile_twomodelblockrouted_pb_t_e_kernel(
         def first_products(u):
             o_ps[u] = []
             for i in range(blocks[u][2]):
-                o = product_banks.tile([P, H], F32, name="o", tag="product")
+                o = o_banks.tile([P, H], F32, name="o")
                 mx_product(o[:], attn_q[u], i, wo_words, wo_planes, blocks[u][0], slice(0, H))
                 o_ps[u].append(o)
 
@@ -228,7 +228,7 @@ def tile_twomodelblockrouted_pb_t_e_kernel(
                 out=mean_eps[:], in0=sumsq[u][:], scalar1=1.0 / H, scalar2=EPS,
                 op0=ALU.mult, op1=ALU.add,
             )
-            rstd[u] = four.tile([P, n], F32, name="rstd")
+            rstd[u] = eight.tile([P, n], F32, name="rstd")
             nc.gpsimd.tensor_tensor(
                 out=rstd[u][:], in0=mean_eps[:], in1=neg_half[:, 0:n], op=ALU.pow
             )
@@ -256,8 +256,8 @@ def tile_twomodelblockrouted_pb_t_e_kernel(
 
         def second_products(u):
             model, unused_tile, n = blocks[u]
-            gate_ps[u] = product_banks.tile([P, n, FF], F32, name="gate", tag="product")
-            up_ps[u] = product_banks.tile([P, n, FF], F32, name="up", tag="product")
+            gate_ps[u] = gu_banks.tile([P, n, FF], F32, name="gate", tag="gu")
+            up_ps[u] = gu_banks.tile([P, n, FF], F32, name="up", tag="gu")
             for out, columns in ((gate_ps[u], slice(0, FF)), (up_ps[u], slice(FF, 2 * FF))):
                 for i in range(n):
                     mx_product(out[:, i, :], h_q[u], i, wgu_words, wgu_planes, model, columns)
@@ -272,6 +272,12 @@ def tile_twomodelblockrouted_pb_t_e_kernel(
             nc.vector.tensor_tensor(out=h_mlp[:], in0=silu_gate[u][:], in1=up_ps[u][:], op=ALU.mult)
             nc.sync.dma_start(out=rows_of(out_1, model, tile, n), in_=h_mlp[:])
 
+        for i in range(WARM_UP):
+            dummy = flipped_banks.tile([P, H], F32, name="dummy", tag="flipped")
+            nc.tensor.matmul(
+                out=dummy[:], lhsT=zeros[:, 0:P], rhs=zeros[:], start=True, stop=True
+            )
+
         def valid(u):
             return 0 <= u < n_blocks
 
@@ -281,30 +287,29 @@ def tile_twomodelblockrouted_pb_t_e_kernel(
         transpose_attn(1)
         regroup_attn(1)
         first_products(0)
-        for model in range(2):
-            spread_ln2(model)
 
-        for t in range(n_blocks + 3):
-            if valid(t - 2):
-                regroup_h(t - 2)
+        for t in range(n_blocks + 5):
+            if t == 1 or t == 8:
+                spread_ln2(t // 8)
             if valid(t - 3):
-                quantise_h(t - 3)
-                second_products(t - 3)
+                normalise(t - 3)
+                transpose_h(t - 3)
+                regroup_h(t - 3)
+            if valid(t - 4):
+                quantise_h(t - 4)
+                second_products(t - 4)
+                silu_of_gate(t - 4)
+            if valid(t - 5):
+                gate_times_up(t - 5)
             if valid(t + 2):
                 transpose_attn(t + 2)
-            if valid(t):
-                add_residual(t)
-                sum_squares(t)
-                reciprocal_rms(t)
-            if valid(t - 3):
-                silu_of_gate(t - 3)
+                regroup_attn(t + 2)
             if valid(t + 1):
                 quantise_attn(t + 1)
+            if valid(t):
+                add_residual(t)
+            if valid(t + 1):
                 first_products(t + 1)
-            if valid(t + 2):
-                regroup_attn(t + 2)
-            if valid(t - 1):
-                normalise(t - 1)
-                transpose_h(t - 1)
-            if valid(t - 3):
-                gate_times_up(t - 3)
+            if valid(t):
+                sum_squares(t)
+                reciprocal_rms(t)

@@ -50,8 +50,9 @@ def tile_twomodelblockrouted_pb_t_e_kernel(
         four = ctx.enter_context(tc.tile_pool(name="four", bufs=4))
         eight = ctx.enter_context(tc.tile_pool(name="eight", bufs=8))
         flipped_banks = ctx.enter_context(tc.psum_pool(name="flipped_banks", bufs=2))
-        o_banks = ctx.enter_context(tc.psum_pool(name="o_banks", bufs=3))
+        o_banks = ctx.enter_context(tc.psum_pool(name="o_banks", bufs=2))
         gu_banks = ctx.enter_context(tc.psum_pool(name="gu_banks", bufs=3))
+        dummy_bank = ctx.enter_context(tc.psum_pool(name="dummy_bank", bufs=1))
 
         ln2_rows = consts.tile([P, H], BF16, name="ln2_rows")
         pick = consts.tile([P, 2, P], BF16, name="pick")
@@ -62,13 +63,13 @@ def tile_twomodelblockrouted_pb_t_e_kernel(
         nc.vector.memset(zeros[:].bitcast(F32), 0.0)
         wo_planes = consts.tile([P, H], U8, name="wo_planes", align_bytes=64)
         nc.vector.memset(wo_planes[:].bitcast(I32), 0)
-        wgu_planes = consts.tile([P, H], U8, name="wgu_planes", align_bytes=64)
-        nc.vector.memset(wgu_planes[:].bitcast(I32), 0)
         nc.vector.memset(ln2_rows[:].bitcast(F32), 0.0)
         nc.vector.memset(pick[:], 0.0)
         for model in range(2):
             row = 32 * model
             nc.vector.memset(pick[row : row + 1, model, :], 1.0)
+        wgu_planes = consts.tile([P, H], U8, name="wgu_planes", align_bytes=64)
+        nc.vector.memset(wgu_planes[:].bitcast(I32), 0)
         neg_half = consts.tile([P, TILES], F32, name="neg_half")
         nc.vector.memset(neg_half[:], -0.5)
         ident = consts.tile([P, P], F32, name="ident")
@@ -105,10 +106,10 @@ def tile_twomodelblockrouted_pb_t_e_kernel(
 
         load_rows(attn, attn_sb, 0, 1, "attn_sb")
         load_rows(attn, attn_sb, 1, 1, "attn_sb")
+        nc.sync.dma_start(out=ln2_rows[0:64:32, :], in_=ln2[:, :])
         load_planes(W_o_scales, wo_planes)
         wo_words[0] = load_words(W_o_words, 0, "wo_words")
         load_rows(x, x_sb, 0, 2, "x_sb")
-        nc.sync.dma_start(out=ln2_rows[0:64:32, :], in_=ln2[:, :])
         load_rows(attn, attn_sb, 2, 1, "attn_sb")
         load_rows(x, x_sb, 2, 1, "x_sb")
         for first in range(3, n_blocks, 2):
@@ -179,12 +180,12 @@ def tile_twomodelblockrouted_pb_t_e_kernel(
         silu_gate = {}
 
         def spread_ln2(model):
-            spread = flipped_banks.tile([P, H], F32, name="spread", tag="flipped")
+            spread = gu_banks.tile([P, H], F32, name="spread", tag="gu")
             nc.tensor.matmul(
                 out=spread[:], lhsT=pick[:, model, :], rhs=ln2_rows[:], start=True, stop=True
             )
             ln2_sb[model] = consts.tile([P, H], BF16, name="ln2_sb%d" % model)
-            nc.vector.tensor_copy(out=ln2_sb[model][:], in_=spread[:])
+            nc.scalar.copy(out=ln2_sb[model][:], in_=spread[:])
 
         def transpose_attn(u):
             flipped[u] = transpose_tiles(attn_sb[u])
@@ -272,25 +273,31 @@ def tile_twomodelblockrouted_pb_t_e_kernel(
             nc.vector.tensor_tensor(out=h_mlp[:], in0=silu_gate[u][:], in1=up_ps[u][:], op=ALU.mult)
             nc.sync.dma_start(out=rows_of(out_1, model, tile, n), in_=h_mlp[:])
 
-        for i in range(WARM_UP):
-            dummy = flipped_banks.tile([P, H], F32, name="dummy", tag="flipped")
+        def valid(u):
+            return 0 <= u < n_blocks
+
+        def keep_clock_up():
+            dummy = dummy_bank.tile([P, H], F32, name="dummy")
             nc.tensor.matmul(
                 out=dummy[:], lhsT=zeros[:, 0:P], rhs=zeros[:], start=True, stop=True
             )
 
-        def valid(u):
-            return 0 <= u < n_blocks
-
-        transpose_attn(0)
-        regroup_attn(0)
+        for i in range(WARM_UP):
+            keep_clock_up()
+        for u in range(2):
+            transpose_attn(u)
+            regroup_attn(u)
+        for model in range(2):
+            spread_ln2(model)
         quantise_attn(0)
-        transpose_attn(1)
-        regroup_attn(1)
         first_products(0)
 
         for t in range(n_blocks + 5):
-            if t == 1 or t == 8:
-                spread_ln2(t // 8)
+            if 1 <= t <= n_blocks + 1:
+                keep_clock_up()
+            if valid(t + 2):
+                transpose_attn(t + 2)
+                regroup_attn(t + 2)
             if valid(t - 3):
                 normalise(t - 3)
                 transpose_h(t - 3)
@@ -301,9 +308,6 @@ def tile_twomodelblockrouted_pb_t_e_kernel(
                 silu_of_gate(t - 4)
             if valid(t - 5):
                 gate_times_up(t - 5)
-            if valid(t + 2):
-                transpose_attn(t + 2)
-                regroup_attn(t + 2)
             if valid(t + 1):
                 quantise_attn(t + 1)
             if valid(t):

@@ -20,7 +20,7 @@ H = 512
 FF = 256
 EPS = 1.1920929e-07
 TILES = 2
-WARM_UP = 4
+WARM_UP = 2
 QUADRANTS = 4
 
 FLOPS = 2 * ROWS * H * H + 2 * ROWS * H * 2 * FF
@@ -178,6 +178,7 @@ def tile_twomodelblockrouted_pb_t_e_kernel(
         gate_ps = {}
         up_ps = {}
         silu_gate = {}
+        up_sb = {}
 
         def spread_ln2(model):
             spread = gu_banks.tile([P, H], F32, name="spread", tag="gu")
@@ -199,7 +200,7 @@ def tile_twomodelblockrouted_pb_t_e_kernel(
         def first_products(u):
             o_ps[u] = []
             for i in range(blocks[u][2]):
-                o = o_banks.tile([P, H], F32, name="o")
+                o = o_banks.tile([P, H], F32, name="o", tag="o")
                 mx_product(o[:], attn_q[u], i, wo_words, wo_planes, blocks[u][0], slice(0, H))
                 o_ps[u].append(o)
 
@@ -267,34 +268,49 @@ def tile_twomodelblockrouted_pb_t_e_kernel(
             silu_gate[u] = four.tile([P, blocks[u][2], FF], F32, name="silu_gate")
             nc.scalar.activation(out=silu_gate[u][:], in_=gate_ps[u][:], func=ACT.Silu)
 
+        def by_gpsimd(u):
+            return u % 2 == 1 and 3 <= u < n_blocks - 3
+
+        def copy_up(u):
+            up_sb[u] = four.tile([P, blocks[u][2], FF], F32, name="up_sb")
+            nc.scalar.copy(out=up_sb[u][:], in_=up_ps[u][:])
+
         def gate_times_up(u):
             model, tile, n = blocks[u]
             h_mlp = whole.tile([P, n, FF], F32, name="h_mlp%d" % u)
-            nc.vector.tensor_tensor(out=h_mlp[:], in0=silu_gate[u][:], in1=up_ps[u][:], op=ALU.mult)
+            if by_gpsimd(u):
+                nc.gpsimd.tensor_tensor(
+                    out=h_mlp[:], in0=silu_gate[u][:], in1=up_sb[u][:], op=ALU.mult
+                )
+            else:
+                nc.vector.tensor_tensor(
+                    out=h_mlp[:], in0=silu_gate[u][:], in1=up_ps[u][:], op=ALU.mult
+                )
             nc.sync.dma_start(out=rows_of(out_1, model, tile, n), in_=h_mlp[:])
 
         def valid(u):
             return 0 <= u < n_blocks
 
-        def keep_clock_up():
-            dummy = dummy_bank.tile([P, H], F32, name="dummy")
+        def keep_clock_up(bank, tag):
+            dummy = bank.tile([P, H], F32, name="dummy", tag=tag)
             nc.tensor.matmul(
                 out=dummy[:], lhsT=zeros[:, 0:P], rhs=zeros[:], start=True, stop=True
             )
 
         for i in range(WARM_UP):
-            keep_clock_up()
+            keep_clock_up(o_banks, "o")
         for u in range(2):
             transpose_attn(u)
             regroup_attn(u)
-        for model in range(2):
-            spread_ln2(model)
+        spread_ln2(0)
         quantise_attn(0)
         first_products(0)
 
         for t in range(n_blocks + 5):
             if 1 <= t <= n_blocks + 1:
-                keep_clock_up()
+                keep_clock_up(dummy_bank, "dummy")
+            if t == 2:
+                spread_ln2(1)
             if valid(t + 2):
                 transpose_attn(t + 2)
                 regroup_attn(t + 2)
@@ -306,7 +322,10 @@ def tile_twomodelblockrouted_pb_t_e_kernel(
                 quantise_h(t - 4)
                 second_products(t - 4)
                 silu_of_gate(t - 4)
-            if valid(t - 5):
+                if by_gpsimd(t - 4):
+                    copy_up(t - 4)
+                    gate_times_up(t - 4)
+            if valid(t - 5) and not by_gpsimd(t - 5):
                 gate_times_up(t - 5)
             if valid(t + 1):
                 quantise_attn(t + 1)

from contextlib import ExitStack

import concourse.mybir as mybir
from concourse.masks import make_identity

F32 = mybir.dt.float32
BF16 = mybir.dt.bfloat16
U8 = mybir.dt.uint8
U32 = mybir.dt.uint32
I32 = mybir.dt.int32
FP8X4 = mybir.dt.float8_e4m3fn_x4
ALU = mybir.AluOpType
ACT = mybir.ActivationFunctionType

P = 128
PACK = 4
ROWS = 4096
ROWS_OF_MODEL = (3072, 1024)
H = 512
FF = 256
EPS = 1.1920929e-07
TILES = 2
WARM_UP = 2
QUADRANTS = 4

FLOPS = 2 * ROWS * H * H + 2 * ROWS * H * 2 * FF


def tile_twomodelblockrouted_pb_t_e_kernel(
    tc, attn, x, W_o_words, W_o_scales, W_gu_words, W_gu_scales, ln2, out_0, out_1
):
    nc = tc.nc

    first_row_of_model = (0, ROWS_OF_MODEL[0])
    blocks = [(0, 0, 1), (0, 1, 1)]
    for model, n_rows in enumerate(ROWS_OF_MODEL):
        for tile in range(2 if model == 0 else 0, n_rows // P, 2):
            blocks.append((model, tile, 2))
    n_blocks = len(blocks)

    def rows_of(dram, model, tile, n_tiles):
        first, n_rows = first_row_of_model[model], ROWS_OF_MODEL[model]
        by_partition = dram[first : first + n_rows, :].rearrange("(p j) n -> p j n", p=P)
        return by_partition[:, tile : tile + n_tiles, :]

    with ExitStack() as ctx:
        ctx.enter_context(tc.manual_schedule())
        consts = ctx.enter_context(tc.tile_pool(name="consts", bufs=1))
        whole = ctx.enter_context(tc.tile_pool(name="whole", bufs=1))
        four = ctx.enter_context(tc.tile_pool(name="four", bufs=4))
        eight = ctx.enter_context(tc.tile_pool(name="eight", bufs=8))
        flipped_banks = ctx.enter_context(tc.psum_pool(name="flipped_banks", bufs=2))
        o_banks = ctx.enter_context(tc.psum_pool(name="o_banks", bufs=2))
        gu_banks = ctx.enter_context(tc.psum_pool(name="gu_banks", bufs=3))
        dummy_bank = ctx.enter_context(tc.psum_pool(name="dummy_bank", bufs=1))

        ln2_rows = consts.tile([P, H], BF16, name="ln2_rows")
        pick = consts.tile([P, 2, P], BF16, name="pick")
        warm = consts.tile([P, 1], F32, name="warm")
        nc.vector.memset(warm[:], 0.0)
        nc.scalar.activation(out=warm[:], in_=warm[:], func=ACT.Silu)
        zeros = consts.tile([P, H], BF16, name="zeros")
        nc.vector.memset(zeros[:].bitcast(F32), 0.0)
        wo_planes = consts.tile([P, H], U8, name="wo_planes", align_bytes=64)
        nc.vector.memset(wo_planes[:].bitcast(I32), 0)
        nc.vector.memset(ln2_rows[:].bitcast(F32), 0.0)
        nc.vector.memset(pick[:], 0.0)
        for model in range(2):
            row = 32 * model
            nc.vector.memset(pick[row : row + 1, model, :], 1.0)
        wgu_planes = consts.tile([P, H], U8, name="wgu_planes", align_bytes=64)
        nc.vector.memset(wgu_planes[:].bitcast(I32), 0)
        neg_half = consts.tile([P, TILES], F32, name="neg_half")
        nc.vector.memset(neg_half[:], -0.5)
        ident = consts.tile([P, P], F32, name="ident")
        make_identity(nc, ident[:])

        attn_sb = {}
        x_sb = {}
        wo_words = {}
        wgu_words = {}

        def load_rows(dram, into, first, n, name):
            model, tile, unused_size = blocks[first]
            n_tiles = sum(size for unused_model, unused_tile, size in blocks[first : first + n])
            loaded = whole.tile([P, n_tiles, H], BF16, name="%s%d" % (name, first))
            nc.sync.dma_start(out=loaded[:], in_=rows_of(dram, model, tile, n_tiles))
            for u in range(first, first + n):
                offset = blocks[u][1] - tile
                into[u] = loaded[:, offset : offset + blocks[u][2], :]

        def load_planes(dram_scales, planes):
            for quadrant in range(QUADRANTS):
                nc.sync.dma_start(
                    out=planes[32 * quadrant : 32 * quadrant + 8, :].bitcast(I32),
                    in_=dram_scales[:, 4 * quadrant : 4 * quadrant + 4, :].bitcast(I32),
                )

        def load_words(dram_words, model, name):
            loaded = consts.tile([P, H], U32, name="%s%d" % (name, model), align_bytes=64)
            nc.sync.dma_start(
                out=loaded[:].bitcast(I32),
                in_=dram_words[model].rearrange("p n t -> p (n t)").bitcast(I32),
            )
            return loaded

        load_rows(attn, attn_sb, 0, 1, "attn_sb")
        load_rows(attn, attn_sb, 1, 1, "attn_sb")
        nc.sync.dma_start(out=ln2_rows[0:64:32, :], in_=ln2[:, :])
        load_planes(W_o_scales, wo_planes)
        wo_words[0] = load_words(W_o_words, 0, "wo_words")
        load_rows(x, x_sb, 0, 2, "x_sb")
        load_rows(attn, attn_sb, 2, 1, "attn_sb")
        load_rows(x, x_sb, 2, 1, "x_sb")
        for first in range(3, n_blocks, 2):
            load_rows(attn, attn_sb, first, 2, "attn_sb")
            if first == 3:
                load_planes(W_gu_scales, wgu_planes)
                wgu_words[0] = load_words(W_gu_words, 0, "wgu_words")
            load_rows(x, x_sb, first, 2, "x_sb")
            if first == 9:
                wo_words[1] = load_words(W_o_words, 1, "wo_words")
                wgu_words[1] = load_words(W_gu_words, 1, "wgu_words")

        def transpose_tiles(row_tiles):
            n = row_tiles.shape[1]
            flipped = flipped_banks.tile([P, n, 2, P], F32, name="flipped", tag="flipped")
            for i in range(n):
                words = row_tiles[:, i, :].bitcast(F32)
                for u in range(2):
                    nc.tensor.transpose(flipped[:, i, u, :], words[:, u : H // 2 : 2], ident[:])
            return flipped

        def regroup(flipped):
            n = flipped.shape[1]
            grouped = four.tile([P, n, P, PACK], BF16, name="grouped", align_bytes=64)
            nc.scalar.copy(
                out=grouped[:].bitcast(F32), in_=flipped[:].rearrange("p i u r -> p i r u")
            )
            return grouped

        def quantise(grouped):
            n = grouped.shape[1]
            codes = four.tile([P, n * P], U32, name="codes", align_bytes=64)
            scales = four.tile([P, n * P], U8, name="scales", align_bytes=64)
            nc.vector.quantize_mx(
                out=codes[:].bitcast(FP8X4),
                scales=scales[:],
                in_=grouped[:].rearrange("p i r t -> p (i r t)"),
            )
            return codes, scales

        def mx_product(out, quantised, i, weight_words, planes, model, columns):
            codes, scales = quantised
            tile_i = slice(i * P, (i + 1) * P)
            nc.tensor.matmul_mx(
                out=out,
                lhsT=codes[:, tile_i].bitcast(FP8X4),
                lhsT_scale=scales[:, tile_i],
                rhs=weight_words[model][:, columns].bitcast(FP8X4),
                rhs_scale=planes[4 * model : P, columns],
                start=True,
                stop=True,
            )

        ln2_sb = {}
        flipped = {}
        attn_grouped = {}
        attn_q = {}
        o_ps = {}
        x_mid = {}
        sumsq = {}
        rstd = {}
        h = {}
        h_flipped = {}
        h_grouped = {}
        h_q = {}
        gate_ps = {}
        up_ps = {}
        silu_gate = {}
        up_sb = {}

        def spread_ln2(model):
            spread = gu_banks.tile([P, H], F32, name="spread", tag="gu")
            nc.tensor.matmul(
                out=spread[:], lhsT=pick[:, model, :], rhs=ln2_rows[:], start=True, stop=True
            )
            ln2_sb[model] = consts.tile([P, H], BF16, name="ln2_sb%d" % model)
            nc.scalar.copy(out=ln2_sb[model][:], in_=spread[:])

        def transpose_attn(u):
            flipped[u] = transpose_tiles(attn_sb[u])

        def regroup_attn(u):
            attn_grouped[u] = regroup(flipped[u])

        def quantise_attn(u):
            attn_q[u] = quantise(attn_grouped[u])

        def first_products(u):
            o_ps[u] = []
            for i in range(blocks[u][2]):
                o = o_banks.tile([P, H], F32, name="o", tag="o")
                mx_product(o[:], attn_q[u], i, wo_words, wo_planes, blocks[u][0], slice(0, H))
                o_ps[u].append(o)

        def add_residual(u):
            model, tile, n = blocks[u]
            x_mid[u] = whole.tile([P, n, H], F32, name="x_mid%d" % u)
            for i in range(n):
                nc.vector.tensor_tensor(
                    out=x_mid[u][:, i, :], in0=o_ps[u][i][:], in1=x_sb[u][:, i, :], op=ALU.add
                )
            nc.sync.dma_start(out=rows_of(out_0, model, tile, n), in_=x_mid[u][:])

        def sum_squares(u):
            n = blocks[u][2]
            sumsq[u] = four.tile([P, n], F32, name="sumsq")
            for i in range(n):
                squares = four.tile([P, H], BF16, name="squares")
                nc.scalar.activation(
                    out=squares[:], in_=x_mid[u][:, i, :], func=ACT.Square,
                    accum_out=sumsq[u][:, i : i + 1],
                )

        def reciprocal_rms(u):
            n = blocks[u][2]
            mean_eps = four.tile([P, n], F32, name="mean_eps")
            nc.gpsimd.tensor_scalar(
                out=mean_eps[:], in0=sumsq[u][:], scalar1=1.0 / H, scalar2=EPS,
                op0=ALU.mult, op1=ALU.add,
            )
            rstd[u] = eight.tile([P, n], F32, name="rstd")
            nc.gpsimd.tensor_tensor(
                out=rstd[u][:], in0=mean_eps[:], in1=neg_half[:, 0:n], op=ALU.pow
            )

        def normalise(u):
            model, unused_tile, n = blocks[u]
            h[u] = four.tile([P, n, H], BF16, name="h")
            for i in range(n):
                nc.vector.scalar_tensor_tensor(
                    out=h[u][:, i, :],
                    in0=x_mid[u][:, i, :],
                    scalar=rstd[u][:, i : i + 1],
                    in1=ln2_sb[model][:],
                    op0=ALU.mult, op1=ALU.mult,
                )

        def transpose_h(u):
            h_flipped[u] = transpose_tiles(h[u])

        def regroup_h(u):
            h_grouped[u] = regroup(h_flipped[u])

        def quantise_h(u):
            h_q[u] = quantise(h_grouped[u])

        def second_products(u):
            model, unused_tile, n = blocks[u]
            gate_ps[u] = gu_banks.tile([P, n, FF], F32, name="gate", tag="gu")
            up_ps[u] = gu_banks.tile([P, n, FF], F32, name="up", tag="gu")
            for out, columns in ((gate_ps[u], slice(0, FF)), (up_ps[u], slice(FF, 2 * FF))):
                for i in range(n):
                    mx_product(out[:, i, :], h_q[u], i, wgu_words, wgu_planes, model, columns)

        def silu_of_gate(u):
            silu_gate[u] = four.tile([P, blocks[u][2], FF], F32, name="silu_gate")
            nc.scalar.activation(out=silu_gate[u][:], in_=gate_ps[u][:], func=ACT.Silu)

        def by_gpsimd(u):
            return u % 2 == 1 and 3 <= u < n_blocks - 3

        def copy_up(u):
            up_sb[u] = four.tile([P, blocks[u][2], FF], F32, name="up_sb")
            nc.scalar.copy(out=up_sb[u][:], in_=up_ps[u][:])

        def gate_times_up(u):
            model, tile, n = blocks[u]
            h_mlp = whole.tile([P, n, FF], F32, name="h_mlp%d" % u)
            if by_gpsimd(u):
                nc.gpsimd.tensor_tensor(
                    out=h_mlp[:], in0=silu_gate[u][:], in1=up_sb[u][:], op=ALU.mult
                )
            else:
                nc.vector.tensor_tensor(
                    out=h_mlp[:], in0=silu_gate[u][:], in1=up_ps[u][:], op=ALU.mult
                )
            nc.sync.dma_start(out=rows_of(out_1, model, tile, n), in_=h_mlp[:])

        def valid(u):
            return 0 <= u < n_blocks

        def keep_clock_up(bank, tag):
            dummy = bank.tile([P, H], F32, name="dummy", tag=tag)
            nc.tensor.matmul(
                out=dummy[:], lhsT=zeros[:, 0:P], rhs=zeros[:], start=True, stop=True
            )

        for i in range(WARM_UP):
            keep_clock_up(o_banks, "o")
        for u in range(2):
            transpose_attn(u)
            regroup_attn(u)
        spread_ln2(0)
        quantise_attn(0)
        first_products(0)

        for t in range(n_blocks + 5):
            if 1 <= t <= n_blocks + 1:
                keep_clock_up(dummy_bank, "dummy")
            if t == 2:
                spread_ln2(1)
            if valid(t + 2):
                transpose_attn(t + 2)
                regroup_attn(t + 2)
            if valid(t - 3):
                normalise(t - 3)
                transpose_h(t - 3)
                regroup_h(t - 3)
            if valid(t - 4):
                quantise_h(t - 4)
                second_products(t - 4)
                silu_of_gate(t - 4)
                if by_gpsimd(t - 4):
                    copy_up(t - 4)
                    gate_times_up(t - 4)
            if valid(t - 5) and not by_gpsimd(t - 5):
                gate_times_up(t - 5)
            if valid(t + 1):
                quantise_attn(t + 1)
            if valid(t):
                add_residual(t)
            if valid(t + 1):
                first_products(t + 1)
            if valid(t):
                sum_squares(t)
                reciprocal_rms(t)
